import numpy as np
import ml_dtypes


def mxq(x, axis, fmt="e4m3"):
    dtype, down = {"e4m3": (ml_dtypes.float8_e4m3fn, 7), "e5m2": (ml_dtypes.float8_e5m2, 14)}[fmt]
    v = np.moveaxis(np.asarray(x, np.float32).astype(ml_dtypes.bfloat16).astype(np.float64), axis, -1)
    blocks = v.reshape(v.shape[:-1] + (-1, 32))
    amax = np.abs(blocks).max(-1, keepdims=True)
    byte = np.maximum(np.where(amax > 0, np.frexp(amax)[1] - 1 + 127, 0) - down, 1)
    scale = np.exp2(byte - 127.0)
    codes = (blocks / scale).astype(np.float32).astype(dtype).astype(np.float64)
    return np.moveaxis((codes * scale).reshape(v.shape), -1, axis)


WIDE = False


def mx_kscale(k):
    if not WIDE:
        return np.ones(k)
    levels = np.array([10, -10, 5, -5, 0])
    if k % 512:
        return np.exp2(np.random.permutation(np.resize(levels, k // 32))).repeat(32)
    a = np.empty((k // 512, 16))
    for p in range(k // 512):
        a[p, :8] = np.random.permutation(np.resize(levels, 8))
        for g in range(8):
            far = levels[np.abs(levels - a[p, g]) >= 10]
            a[p, g + 8] = far[np.random.randint(len(far))]
    return np.exp2(a.ravel()).repeat(32)


BF16 = ml_dtypes.bfloat16


def bf(x):
    return np.asarray(x, np.float32).astype(BF16)


def f64(x):
    return np.asarray(x).astype(np.float64)


B, T, U, D_ENC, D_PRED, D_JOINT, VOCAB = 4, 128, 32, 512, 512, 512, 128
LOGIT_CLAMP = 15.0


def draw0():
    se, sp = mx_kscale(D_ENC), mx_kscale(D_PRED)
    t = mx_kscale(D_JOINT)
    g = t / t.max()
    return {"encoder_out": bf(np.random.standard_normal((B, T, D_ENC)) * se),
            "predictor_out": bf(np.random.standard_normal((B, U, D_PRED)) * sp),
            "W_enc": bf(np.random.standard_normal((D_ENC, D_JOINT)) * 0.7 / np.sqrt(D_ENC) / se[:, None] * g),
            "b_enc": bf(np.random.standard_normal(D_JOINT) * 0.2 * g),
            "W_pred": bf(np.random.standard_normal((D_PRED, D_JOINT)) * 0.7 / np.sqrt(D_PRED) / sp[:, None] * g),
            "b_pred": bf(np.random.standard_normal(D_JOINT) * 0.2 * g),
            "W_out": bf(np.random.standard_normal((D_JOINT, VOCAB)) * 8.0 / np.sqrt(D_JOINT) / g[:, None]),
            "b_out": bf(np.random.standard_normal(VOCAB) * 0.5)}


def core(encoder_out, predictor_out, W_enc, b_enc, W_pred, b_pred, W_out, b_out):
    enc = (mxq(f64(encoder_out), 2, "e4m3") @ mxq(f64(W_enc), 0, "e4m3")) + f64(b_enc)
    pred = (mxq(f64(predictor_out), 2, "e4m3") @ mxq(f64(W_pred), 0, "e4m3")) + f64(b_pred)
    joint = np.tanh(enc[:, :, None, :] + pred[:, None, :, :])
    logits = (mxq(joint, 3, "e4m3") @ mxq(f64(W_out), 0, "e4m3")) + f64(b_out)
    return np.clip(logits, -LOGIT_CLAMP, LOGIT_CLAMP)


def e4m3fn_bytes(y):
    return np.clip(np.asarray(y, np.float64), -448.0, 448.0).astype(np.float32).astype(ml_dtypes.float8_e4m3fn).view(np.uint8)


def e4m3fn_values(b):
    return np.asarray(b, np.uint8).view(ml_dtypes.float8_e4m3fn).astype(np.float64)


def setup_inputs():
    d = draw0()
    x0 = np.asarray(d['encoder_out']).astype(np.float64)
    s = (np.max(np.abs(x0), axis=(0, 1), keepdims=True) / 448.0).astype(np.float32)
    out = {}
    for k, v in d.items():
        if k == 'encoder_out':
            out['encoder_out_bytes'] = e4m3fn_bytes(x0 / s.astype(np.float64))
            out['encoder_out_scale'] = s
        else:
            out[k] = v
    return out


def reference(encoder_out_bytes, encoder_out_scale, predictor_out, W_enc, b_enc, W_pred, b_pred, W_out, b_out):
    return core(e4m3fn_values(encoder_out_bytes) * encoder_out_scale.astype(np.float64), predictor_out, W_enc, b_enc, W_pred, b_pred, W_out, b_out)

@@ -1,0 +1,219 @@
+from contextlib import ExitStack
+
+import concourse.mybir as mybir
+from concourse.masks import make_identity
+
+F32 = mybir.dt.float32
+BF16 = mybir.dt.bfloat16
+U32 = mybir.dt.uint32
+U8 = mybir.dt.uint8
+FP8 = mybir.dt.float8_e4m3fn
+FP8X4 = mybir.dt.float8_e4m3fn_x4
+ALU = mybir.AluOpType
+ACT = mybir.ActivationFunctionType
+
+P = 128
+J = 4
+B, T, U, K, V = 4, 128, 32, 512, 128
+LIMIT = 15.0
+FLOPS = 2 * (B * T * K * K + B * U * K * K + B * T * U * K * V)
+
+
+def tile_jointnetwork_t_kernel(tc, x_bytes, x_scale, pred, w_enc, b_enc, w_pred, b_pred, w_out, b_out, out):
+    nc = tc.nc
+    sizes = {b: [4] * 8 for b in range(B)}
+    sizes[0] = [1,1,2,4,4,4,4,4,4,4]
+    sizes[B - 1] = [4,4,4,4,4,4,4,2,1,1]
+    groups = []
+    for b in range(B):
+        u = 0
+        for n in sizes[b]:
+            groups.append((b, u, n))
+            u += n
+    ngroups = len(groups)
+    first_group = [min(i for i in range(ngroups) if groups[i][0] == b) for b in range(B)]
+
+    with ExitStack() as ctx:
+        keep = ctx.enter_context(tc.tile_pool(name="keep", bufs=1))
+        stage = ctx.enter_context(tc.tile_pool(name="stage", bufs=3))
+        psum = ctx.enter_context(tc.psum_pool(name="psum", bufs=1))
+        ctx.enter_context(tc.manual_schedule())
+
+        scale = keep.tile([P, J], F32, name="scale")
+        nc.sync.dma_start(out=scale[:], in_=x_scale.rearrange("o q (p j) -> p (o q j)", j=J))
+        bytes_in = keep.tile([P, B, K], U8, name="bytes_in", align_bytes=64)
+        nc.sync.dma_start(out=bytes_in[:], in_=x_bytes.rearrange("b t k -> t b k"))
+        pred_sb = keep.tile([P, K], BF16, name="pred_sb", align_bytes=64)
+        nc.sync.dma_start(out=pred_sb[:], in_=pred.rearrange("b u k -> (b u) k"))
+        we_raw = keep.tile([P, J, K], BF16, name="we_raw", align_bytes=64)
+        nc.sync.dma_start(out=we_raw[:], in_=w_enc.rearrange("(p j) c -> p j c", j=J))
+        wp_raw = keep.tile([P, J, K], BF16, name="wp_raw", align_bytes=64)
+        nc.sync.dma_start(out=wp_raw[:], in_=w_pred.rearrange("(p j) c -> p j c", j=J))
+        wo_raw = keep.tile([P, J, V], BF16, name="wo_raw", align_bytes=64)
+        nc.sync.dma_start(out=wo_raw[:], in_=w_out.rearrange("(p j) v -> p j v", j=J))
+        be = keep.tile([P, J], BF16, name="be")
+        nc.gpsimd.dma_start(out=be[:], in_=b_enc.rearrange("(p j) -> p j", j=J))
+        bp = keep.tile([P, J], BF16, name="bp")
+        nc.gpsimd.dma_start(out=bp[:], in_=b_pred.rearrange("(p j) -> p j", j=J))
+        bo = keep.tile([P, V], BF16, name="bo")
+
+        ident = keep.tile([P, P], F32, name="ident", align_bytes=64)
+        make_identity(nc, ident[:])
+        nc.gpsimd.dma_start(out=bo[:], in_=b_out.partition_broadcast(P))
+
+        warm = keep.tile([P, 1], F32, name="warm")
+        nc.vector.memset(warm[:], 0.0)
+        warm2 = keep.tile([P, 1], F32, name="warm2")
+        nc.scalar.activation(out=warm2[:], in_=warm[:], func=ACT.Tanh)
+
+        we_int = keep.tile([P, J, P, J], BF16, name="we_int", align_bytes=64)
+        we_c = keep.tile([P, J, P], U32, name="we_c", align_bytes=64)
+        we_s = keep.tile([P, J, P], U8, name="we_s", align_bytes=64)
+        wp_int = keep.tile([P, J, P, J], BF16, name="wp_int", align_bytes=64)
+        wp_c = keep.tile([P, J, P], U32, name="wp_c", align_bytes=64)
+        wp_s = keep.tile([P, J, P], U8, name="wp_s", align_bytes=64)
+        wo_int = keep.tile([P, V, J], BF16, name="wo_int", align_bytes=64)
+        wo_c = keep.tile([P, V], U32, name="wo_c", align_bytes=64)
+        wo_s = keep.tile([P, V], U8, name="wo_s", align_bytes=64)
+        bsum = keep.tile([P, J], F32, name="bsum")
+        pred_b = keep.tile([P, J, P], F32, name="pred_b", align_bytes=64)
+        pred_int = keep.tile([P, P, J], BF16, name="pred_int", align_bytes=64)
+        pred_c = keep.tile([P, P], U32, name="pred_c", align_bytes=64)
+        pred_s = keep.tile([P, P], U8, name="pred_s", align_bytes=64)
+        x_bf = keep.tile([P, B, K], BF16, name="x_bf", align_bytes=64)
+        x_int = [keep.tile([P, P, J], BF16, name="x_int%d" % b, align_bytes=64) for b in range(B)]
+        x_c = [keep.tile([P, P], U32, name="x_c%d" % b, align_bytes=64) for b in range(B)]
+        x_s = [keep.tile([P, P], U8, name="x_s%d" % b, align_bytes=64) for b in range(B)]
+        enc_ps = [None] * B
+
+        def turn(src, name):
+            xt = psum.tile([P, 2, P], F32, name=name, tag="xt", bufs=2)
+            words = src.bitcast(F32)
+            for w in range(2):
+                nc.tensor.transpose(xt[:, w, :], words[:, w:2 * P:2], ident[:])
+            return xt
+
+        def w_plane(engine_copy, raw, dst, t):
+            engine_copy(out=dst[:, t], in_=raw[:].rearrange("p j (m t) -> p t m j", t=J)[:, t])
+
+        def quant(c, s, src):
+            nc.vector.quantize_mx(out=c.bitcast(FP8X4), scales=s, in_=src)
+
+        def x_product(b, xt):
+            nc.vector.tensor_tensor(
+                out=x_int[b][:].rearrange("p r (w e) -> p r w e", e=2),
+                in0=xt[:].rearrange("p w r -> p (w r)").bitcast(BF16).rearrange("p (w r e) -> p r w e", w=2, e=2),
+                in1=scale[:].rearrange("p (w e) -> p w e", e=2).unsqueeze(1).to_broadcast([P, P, 2, 2]),
+                op=ALU.mult,
+            )
+
+        def x_quant(b):
+            quant(x_c[b][:], x_s[b][:], x_int[b][:].rearrange("p r j -> p (r j)"))
+
+        def mx(ps, t, wc, ws, c, s):
+            nc.tensor.matmul_mx(out=ps[:, t, :], lhsT=wc[:, t, :].bitcast(FP8X4), lhsT_scale=ws[:, t, :],
+                                rhs=c.bitcast(FP8X4), rhs_scale=s, start=True, stop=True)
+
+        def x_matmul(b):
+            enc_ps[b] = psum.tile([P, J, P], F32, name="enc%d" % b, tag="enc", bufs=2)
+            for t in range(J):
+                mx(enc_ps[b], t, we_c, we_s, x_c[b][:], x_s[b][:])
+
+        nc.scalar.copy(out=x_bf[:, 0, :], in_=bytes_in[:, 0, :].bitcast(FP8))
+        nc.scalar.copy(out=x_bf[:, 1:, :].rearrange("p b k -> p (b k)"), in_=bytes_in[:, 1:, :].rearrange("p b k -> p (b k)").bitcast(FP8))
+        xt0 = turn(x_bf[:, 0, :], "xt0")
+        x_product(0, xt0)
+        xtp = turn(pred_sb[:], "xtp")
+        nc.vector.tensor_tensor(out=bsum[:], in0=be[:], in1=bp[:], op=ALU.add)
+        x_quant(0)
+        nc.scalar.copy(out=pred_int[:].rearrange("p r j -> p (r j)").bitcast(F32).rearrange("p (r w) -> p r w", w=2), in_=xtp[:].rearrange("p w r -> p r w"))
+        w_plane(nc.vector.tensor_copy, we_raw, we_int, 0)
+        w_plane(nc.vector.tensor_copy, we_raw, we_int, 1)
+        w_plane(nc.scalar.copy, we_raw, we_int, 2)
+        w_plane(nc.scalar.copy, we_raw, we_int, 3)
+        quant(we_c[:, 0, :], we_s[:, 0, :], we_int[:, 0].rearrange("p m j -> p (m j)"))
+        quant(pred_c[:], pred_s[:], pred_int[:].rearrange("p r j -> p (r j)"))
+        quant(we_c[:, 1, :], we_s[:, 1, :], we_int[:, 1].rearrange("p m j -> p (m j)"))
+        w_plane(nc.vector.tensor_copy, wp_raw, wp_int, 0)
+        w_plane(nc.vector.tensor_copy, wp_raw, wp_int, 1)
+        w_plane(nc.scalar.copy, wp_raw, wp_int, 3)
+        quant(we_c[:, 2, :], we_s[:, 2, :], we_int[:, 2].rearrange("p m j -> p (m j)"))
+        quant(wp_c[:, 0, :], wp_s[:, 0, :], wp_int[:, 0].rearrange("p m j -> p (m j)"))
+        w_plane(nc.vector.tensor_copy, wp_raw, wp_int, 2)
+        quant(we_c[:, 3, :], we_s[:, 3, :], we_int[:, 3].rearrange("p m j -> p (m j)"))
+        quant(wp_c[:, 1, :], wp_s[:, 1, :], wp_int[:, 1].rearrange("p m j -> p (m j)"))
+        quant(wp_c[:, 2, :], wp_s[:, 2, :], wp_int[:, 2].rearrange("p m j -> p (m j)"))
+        quant(wp_c[:, 3, :], wp_s[:, 3, :], wp_int[:, 3].rearrange("p m j -> p (m j)"))
+        x_matmul(0)
+        pp = psum.tile([P, J, P], F32, name="pp", tag="pp", bufs=1)
+        for t in range(J):
+            mx(pp, t, wp_c, wp_s, pred_c[:], pred_s[:])
+        nc.vector.tensor_tensor(out=pred_b[:], in0=pp[:], in1=bsum[:].unsqueeze(2).to_broadcast([P, J, P]), op=ALU.add)
+        nc.vector.tensor_copy(out=wo_int[:], in_=wo_raw[:].rearrange("p j v -> p v j"))
+
+        planes, inter, codes, scales, acc, res = {}, {}, {}, {}, {}, {}
+
+        def tanh_group(i):
+            b, u0, n = groups[i]
+            planes[i] = stage.tile([P, J, 4, T], BF16, name="planes", tag="planes", bufs=3, align_bytes=64)
+            for u in range(n):
+                for j in range(J):
+                    nc.scalar.activation(out=planes[i][:, j, u, :], in_=enc_ps[b][:, j, :], func=ACT.Tanh,
+                                         bias=pred_b[:, j, b * U + u0 + u:b * U + u0 + u + 1])
+
+        def interleave(i):
+            n = groups[i][2]
+            inter[i] = stage.tile([P, 4 * T, J], BF16, name="inter", tag="inter", bufs=2, align_bytes=64)
+            dst = inter[i][:, :n * T, :]
+            src = planes[i][:].rearrange("p j u t -> p j (u t)")[:, :, :n * T]
+            nc.vector.tensor_copy(out=dst.rearrange("p (c i) j -> p c j i", i=4), in_=src.rearrange("p j (c i) -> p c j i", i=4))
+
+        def quantise(i):
+            n = groups[i][2]
+            codes[i] = stage.tile([P, 4 * T], U32, name="codes", tag="codes", bufs=3, align_bytes=64)
+            scales[i] = stage.tile([P, 4 * T], U8, name="scales", tag="scales", bufs=3, align_bytes=64)
+            quant(codes[i][:, :n * T], scales[i][:, :n * T], inter[i][:, :n * T, :].rearrange("p c j -> p (c j)"))
+
+        def multiply(i):
+            n = groups[i][2]
+            acc[i] = psum.tile([P, 4, V], F32, name="acc", tag="acc", bufs=3)
+            for u in range(n):
+                cols = slice(u * T, (u + 1) * T)
+                nc.tensor.matmul_mx(out=acc[i][:, u, :], lhsT=codes[i][:, cols].bitcast(FP8X4), lhsT_scale=scales[i][:, cols],
+                                    rhs=wo_c[:].bitcast(FP8X4), rhs_scale=wo_s[:], start=True, stop=True)
+
+        def add_bias(i):
+            n = groups[i][2]
+            res[i] = stage.tile([P, 4, V], F32, name="res", tag="res", bufs=4, align_bytes=64)
+            nc.vector.tensor_tensor(out=res[i][:, :n, :], in0=acc[i][:, :n, :], in1=bo[:].unsqueeze(1).to_broadcast([P, n, V]), op=ALU.add)
+
+        def clip_store(i):
+            b, u0, n = groups[i]
+            nc.vector.tensor_scalar(out=res[i][:, :n, :], in0=res[i][:, :n, :], scalar1=LIMIT, scalar2=-LIMIT, op0=ALU.min, op1=ALU.max)
+            nc.sync.dma_start(out=out[b, :, u0:u0 + n, :], in_=res[i][:, :n, :])
+
+        xts = {}
+        x_at = {}
+        for b in range(1, B):
+            x_at.setdefault(first_group[b - 1] + 2, []).append(b)
+        for i in range(ngroups + 3):
+            if i < ngroups:
+                tanh_group(i)
+            for b in x_at.get(i, []):
+                xts[b] = turn(x_bf[:, b, :], "xt%d" % b)
+                x_product(b, xts[b])
+            if 0 <= i - 1 < ngroups:
+                interleave(i - 1)
+            if i == 1:
+                quant(wo_c[:], wo_s[:], wo_int[:].rearrange("p v j -> p (v j)"))
+            if 0 <= i - 2 < ngroups:
+                add_bias(i - 2)
+            if 0 <= i - 1 < ngroups:
+                quantise(i - 1)
+            for b in x_at.get(i, []):
+                x_quant(b)
+                x_matmul(b)
+            if 0 <= i - 1 < ngroups:
+                multiply(i - 1)
+            if 0 <= i - 2 < ngroups:
+                clip_store(i - 2)

@@ -17,21 +17,30 @@ J = 4
 B, T, U, K, V = 4, 128, 32, 512, 128
 LIMIT = 15.0
 FLOPS = 2 * (B * T * K * K + B * U * K * K + B * T * U * K * V)
+LOOK = 6
+HEAD = 20
 
 
 def tile_jointnetwork_t_kernel(tc, x_bytes, x_scale, pred, w_enc, b_enc, w_pred, b_pred, w_out, b_out, out):
     nc = tc.nc
-    sizes = {b: [4] * 8 for b in range(B)}
-    sizes[0] = [1,1,2,4,4,4,4,4,4,4]
-    sizes[B - 1] = [4,4,4,4,4,4,4,2,1,1]
-    groups = []
-    for b in range(B):
+    ugroups = []
+    for b in range(2):
         u = 0
-        for n in sizes[b]:
-            groups.append((b, u, n))
+        for n in ([1,1,2,4,4,4,4,4,4,4] if b == 0 else [4,4,4,4,4,4,4,4]):
+            ugroups.append(("u", b, 0, u, n))
             u += n
+    tgroups = [("t", 2 + i // 8, i % 8, 0, 4) for i in range(15)]
+    for s0, n in ((0,2),(2,1),(3,1)):
+        tgroups.append(("t", 3, 7, s0, n))
+    groups = ugroups + tgroups
     ngroups = len(groups)
-    first_group = [min(i for i in range(ngroups) if groups[i][0] == b) for b in range(B)]
+    uunits = [(i, x) for i in range(len(ugroups)) for x in range(groups[i][4])]
+    tunits = [(i, x) for i in range(len(ugroups), ngroups) for x in range(groups[i][4])]
+    units = uunits[:HEAD]
+    rest = uunits[HEAD:]
+    for n in range(len(tunits)):
+        units.append(tunits[n])
+        units.extend(rest[n * len(rest) // len(tunits):(n + 1) * len(rest) // len(tunits)])
 
     with ExitStack() as ctx:
         keep = ctx.enter_context(tc.tile_pool(name="keep", bufs=1))
@@ -84,10 +93,14 @@ def tile_jointnetwork_t_kernel(tc, x_bytes, x_scale, pred, w_enc, b_enc, w_pred,
         x_int = [keep.tile([P, P, J], BF16, name="x_int%d" % b, align_bytes=64) for b in range(B)]
         x_c = [keep.tile([P, P], U32, name="x_c%d" % b, align_bytes=64) for b in range(B)]
         x_s = [keep.tile([P, P], U8, name="x_s%d" % b, align_bytes=64) for b in range(B)]
+        p_nat = keep.tile([P, K], F32, name="p_nat", align_bytes=64)
+        e_nat = {b: keep.tile([P, K], F32, name="e_nat%d" % b, align_bytes=64) for b in (2, 3)}
+        e_rep = {b: [keep.tile([P, 2, K], F32, name="e_rep%d%d" % (b, h), align_bytes=64) for h in range(4)] for b in (2, 3)}
+        p_rep = {b: keep.tile([P, 4, K], F32, name="p_rep%d" % b, align_bytes=64) for b in (2, 3)}
         enc_ps = [None] * B
 
         def turn(src, name):
-            xt = psum.tile([P, 2, P], F32, name=name, tag="xt", bufs=2)
+            xt = psum.tile([P, 2, P], F32, name=name, tag="sum", bufs=4)
             words = src.bitcast(F32)
             for w in range(2):
                 nc.tensor.transpose(xt[:, w, :], words[:, w:2 * P:2], ident[:])
@@ -119,6 +132,9 @@ def tile_jointnetwork_t_kernel(tc, x_bytes, x_scale, pred, w_enc, b_enc, w_pred,
             for t in range(J):
                 mx(enc_ps[b], t, we_c, we_s, x_c[b][:], x_s[b][:])
 
+        def scratch(q):
+            return out[B - 1, 16 * q:16 * (q + 1), :, :].rearrange("t (a c) v -> (t a) (c v)", c=4)
+
         nc.scalar.copy(out=x_bf[:, 0, :], in_=bytes_in[:, 0, :].bitcast(FP8))
         nc.scalar.copy(out=x_bf[:, 1:, :].rearrange("p b k -> p (b k)"), in_=bytes_in[:, 1:, :].rearrange("p b k -> p (b k)").bitcast(FP8))
         xt0 = turn(x_bf[:, 0, :], "xt0")
@@ -145,75 +161,144 @@ def tile_jointnetwork_t_kernel(tc, x_bytes, x_scale, pred, w_enc, b_enc, w_pred,
         quant(wp_c[:, 2, :], wp_s[:, 2, :], wp_int[:, 2].rearrange("p m j -> p (m j)"))
         quant(wp_c[:, 3, :], wp_s[:, 3, :], wp_int[:, 3].rearrange("p m j -> p (m j)"))
         x_matmul(0)
-        pp = psum.tile([P, J, P], F32, name="pp", tag="pp", bufs=1)
+        pp = psum.tile([P, J, P], F32, name="pp", tag="sum", bufs=4)
         for t in range(J):
             mx(pp, t, wp_c, wp_s, pred_c[:], pred_s[:])
         nc.vector.tensor_tensor(out=pred_b[:], in0=pp[:], in1=bsum[:].unsqueeze(2).to_broadcast([P, J, P]), op=ALU.add)
+        pn = psum.tile([P, J, P], F32, name="pn", tag="sum", bufs=4)
+        xt2 = turn(x_bf[:, 2, :], "xt2")
+        for t in range(J):
+            nc.tensor.transpose(pn[:, t, :], pred_b[:, t, :], ident[:])
+        x_product(2, xt2)
+        nc.vector.tensor_copy(out=p_nat[:], in_=pn[:].rearrange("p j m -> p (j m)"))
+        nc.sync.dma_start(out=scratch(5), in_=p_nat[:])
+        x_quant(2)
         nc.vector.tensor_copy(out=wo_int[:], in_=wo_raw[:].rearrange("p j v -> p v j"))
 
-        planes, inter, codes, scales, acc, res = {}, {}, {}, {}, {}, {}
+        def natural(b):
+            en = psum.tile([P, K], F32, name="en%d" % b, tag="sum", bufs=4)
+            nc.tensor.matmul_mx(out=en[:], lhsT=x_c[b][:].bitcast(FP8X4), lhsT_scale=x_s[b][:],
+                                rhs=we_c[:].rearrange("p t m -> p (t m)").bitcast(FP8X4), rhs_scale=we_s[:].rearrange("p t m -> p (t m)"), start=True, stop=True)
+            nc.vector.tensor_copy(out=e_nat[b][:], in_=en[:])
+            nc.sync.dma_start(out=scratch(4 + b), in_=e_nat[b][:])
 
-        def tanh_group(i):
-            b, u0, n = groups[i]
-            planes[i] = stage.tile([P, J, 4, T], BF16, name="planes", tag="planes", bufs=3, align_bytes=64)
-            for u in range(n):
+        ORDER = (0, 4, 1, 5, 2, 6, 3, 7)
+
+        def rep_p(b):
+            rows = scratch(5).rearrange("(b ul s) k -> b ul (s k)", b=B, s=4)
+            for ul in ORDER:
+                nc.sync.dma_start(out=p_rep[b][ul:P:8].rearrange("p s k -> p (s k)"), in_=rows[b, ul].partition_broadcast(16))
+
+        def rep_e(b, h):
+            for ul in ORDER:
+                nc.sync.dma_start(out=e_rep[b][h][ul:P:8], in_=scratch(4 + b).rearrange("(tb tl) k -> tl tb k", tl=16)[:, 2 * h:2 * h + 2])
+
+        planes, inter, codes, scales, acc, res, sums = {}, {}, {}, {}, {}, {}, {}
+
+        def sum_unit(q):
+            i, x = units[q]
+            kind, b, tb, s0, n = groups[i]
+            if kind == "u":
+                return
+            s = s0 + x
+            sums[q] = psum.tile([P, J, P], F32, name="sums", tag="sum", bufs=4)
+            for j in range(J):
+                cols = slice(j * P, (j + 1) * P)
+                nc.tensor.matmul(sums[q][:, j, :], lhsT=e_rep[b][tb // 2][:, tb % 2, cols], rhs=ident[:], start=True, stop=False, is_transpose=True)
+                nc.tensor.matmul(sums[q][:, j, :], lhsT=p_rep[b][:, s, cols], rhs=ident[:], start=False, stop=True, is_transpose=True)
+
+        def tanh_unit(q):
+            i, x = units[q]
+            kind, b, tb, u0, n = groups[i]
+            if kind == "u":
+                if x == 0:
+                    planes[i] = stage.tile([P, J, 4, T], BF16, name="planes", tag="planes", bufs=3, align_bytes=64)
                 for j in range(J):
-                    nc.scalar.activation(out=planes[i][:, j, u, :], in_=enc_ps[b][:, j, :], func=ACT.Tanh,
-                                         bias=pred_b[:, j, b * U + u0 + u:b * U + u0 + u + 1])
+                    nc.scalar.activation(out=planes[i][:, j, x, :], in_=enc_ps[b][:, j, :], func=ACT.Tanh,
+                                         bias=pred_b[:, j, b * U + u0 + x:b * U + u0 + x + 1])
+            else:
+                if x == 0:
+                    inter[i] = stage.tile([P, 4 * T, J], BF16, name="inter", tag="inter", bufs=4, align_bytes=64)
+                nc.scalar.activation(out=inter[i][:, x * T:(x + 1) * T, :], in_=sums[q][:].rearrange("p j n -> p n j"), func=ACT.Tanh)
 
         def interleave(i):
-            n = groups[i][2]
-            inter[i] = stage.tile([P, 4 * T, J], BF16, name="inter", tag="inter", bufs=2, align_bytes=64)
+            kind, b, tb, u0, n = groups[i]
+            if kind == "t":
+                return
+            inter[i] = stage.tile([P, 4 * T, J], BF16, name="inter", tag="inter", bufs=4, align_bytes=64)
             dst = inter[i][:, :n * T, :]
             src = planes[i][:].rearrange("p j u t -> p j (u t)")[:, :, :n * T]
             nc.vector.tensor_copy(out=dst.rearrange("p (c i) j -> p c j i", i=4), in_=src.rearrange("p j (c i) -> p c j i", i=4))
 
         def quantise(i):
-            n = groups[i][2]
+            n = groups[i][4]
             codes[i] = stage.tile([P, 4 * T], U32, name="codes", tag="codes", bufs=3, align_bytes=64)
             scales[i] = stage.tile([P, 4 * T], U8, name="scales", tag="scales", bufs=3, align_bytes=64)
             quant(codes[i][:, :n * T], scales[i][:, :n * T], inter[i][:, :n * T, :].rearrange("p c j -> p (c j)"))
 
         def multiply(i):
-            n = groups[i][2]
-            acc[i] = psum.tile([P, 4, V], F32, name="acc", tag="acc", bufs=3)
+            n = groups[i][4]
+            acc[i] = psum.tile([P, 4, V], F32, name="acc", tag="acc", bufs=2)
             for u in range(n):
                 cols = slice(u * T, (u + 1) * T)
                 nc.tensor.matmul_mx(out=acc[i][:, u, :], lhsT=codes[i][:, cols].bitcast(FP8X4), lhsT_scale=scales[i][:, cols],
                                     rhs=wo_c[:].bitcast(FP8X4), rhs_scale=wo_s[:], start=True, stop=True)
 
         def add_bias(i):
-            n = groups[i][2]
+            n = groups[i][4]
             res[i] = stage.tile([P, 4, V], F32, name="res", tag="res", bufs=4, align_bytes=64)
             nc.vector.tensor_tensor(out=res[i][:, :n, :], in0=acc[i][:, :n, :], in1=bo[:].unsqueeze(1).to_broadcast([P, n, V]), op=ALU.add)
 
         def clip_store(i):
-            b, u0, n = groups[i]
+            kind, b, tb, u0, n = groups[i]
             nc.vector.tensor_scalar(out=res[i][:, :n, :], in0=res[i][:, :n, :], scalar1=LIMIT, scalar2=-LIMIT, op0=ALU.min, op1=ALU.max)
-            nc.sync.dma_start(out=out[b, :, u0:u0 + n, :], in_=res[i][:, :n, :])
+            if kind == "u":
+                dst = out[b, :, u0:u0 + n, :]
+            else:
+                dst = out[b, 16 * tb:16 * (tb + 1), :, :].rearrange("t (a c) v -> (t a) c v", c=4)[:, u0:u0 + n, :]
+            nc.sync.dma_start(out=dst, in_=res[i][:, :n, :])
 
-        xts = {}
-        x_at = {}
-        for b in range(1, B):
-            x_at.setdefault(first_group[b - 1] + 2, []).append(b)
-        for i in range(ngroups + 3):
-            if i < ngroups:
-                tanh_group(i)
-            for b in x_at.get(i, []):
-                xts[b] = turn(x_bf[:, b, :], "xt%d" % b)
-                x_product(b, xts[b])
-            if 0 <= i - 1 < ngroups:
-                interleave(i - 1)
-            if i == 1:
-                quant(wo_c[:], wo_s[:], wo_int[:].rearrange("p v j -> p (v j)"))
-            if 0 <= i - 2 < ngroups:
-                add_bias(i - 2)
-            if 0 <= i - 1 < ngroups:
-                quantise(i - 1)
-            for b in x_at.get(i, []):
-                x_quant(b)
-                x_matmul(b)
-            if 0 <= i - 1 < ngroups:
-                multiply(i - 1)
-            if 0 <= i - 2 < ngroups:
-                clip_store(i - 2)
+        def side(b):
+            xtb = turn(x_bf[:, b, :], "xt%d" % b)
+            x_product(b, xtb)
+
+        slots = {}
+
+        def at(slot, order, *task):
+            slots.setdefault(slot, []).append((order, len(slots.get(slot, [])), task))
+
+        at(0, 0, natural, 2)
+        at(0, 1, rep_p, 2)
+        at(0, 2, rep_e, 2, 0)
+        at(1, 0, side, 3)
+        at(2, 0, x_quant, 3)
+        at(2, 1, natural, 3)
+        at(4, 0, side, 1)
+        at(5, 0, x_quant, 1)
+        at(5, 1, x_matmul, 1)
+        at(1, 5, lambda z: quant(wo_c[:], wo_s[:], wo_int[:].rearrange("p v j -> p (v j)")), 0)
+        sumq = [q for q in range(len(units)) if groups[units[q][0]][0] == "t"]
+        for h in range(1, 8):
+            b = 2 + h // 4
+            slot = max(3, sumq[8 * h] - 16)
+            if h == 4:
+                at(slot, 6, rep_p, b)
+            at(slot, 7, rep_e, b, h % 4)
+        done = 0
+        for q in range(len(units) + 8):
+            if q < len(units):
+                i, x = units[q]
+                while done < len(sumq) and sumq[done] <= q + LOOK:
+                    sum_unit(sumq[done])
+                    done += 1
+                tanh_unit(q)
+                if x == groups[i][4] - 1:
+                    late = 1 if groups[i][0] == "u" else 0
+                    if late:
+                        at(q + 1, 2, interleave, i)
+                    at(q + 1 + late, 3, quantise, i)
+                    at(q + 1 + late, 4, multiply, i)
+                    at(q + 3 + late, 1, add_bias, i)
+                    at(q + 3 + 1 + late, 0, clip_store, i)
+            for order, seq, task in sorted(slots.get(q, []), key=lambda z: z[:2]):
+                task[0](*task[1:])

@@ -18,19 +18,20 @@ B, T, U, K, V = 4, 128, 32, 512, 128
 LIMIT = 15.0
 FLOPS = 2 * (B * T * K * K + B * U * K * K + B * T * U * K * V)
 LOOK = 6
-HEAD = 20
+HEAD = 24
 
 
 def tile_jointnetwork_t_kernel(tc, x_bytes, x_scale, pred, w_enc, b_enc, w_pred, b_pred, w_out, b_out, out):
     nc = tc.nc
+    sizes = [[1, 1, 2, 4, 4, 4, 4, 4, 4, 4], [4] * 8, [4] * 7 + [2, 1, 1]]
     ugroups = []
-    for b in range(2):
+    for b in range(3):
         u = 0
-        for n in ([1,1,2,4,4,4,4,4,4,4] if b == 0 else [4,4,4,4,4,4,4,4]):
+        for n in sizes[b]:
             ugroups.append(("u", b, 0, u, n))
             u += n
-    tgroups = [("t", 2 + i // 8, i % 8, 0, 4) for i in range(15)]
-    for s0, n in ((0,2),(2,1),(3,1)):
+    tgroups = [("t", 3, i, 0, 4) for i in range(7)]
+    for s0, n in ((0, 2), (2, 1), (3, 1)):
         tgroups.append(("t", 3, 7, s0, n))
     groups = ugroups + tgroups
     ngroups = len(groups)
@@ -39,8 +40,8 @@ def tile_jointnetwork_t_kernel(tc, x_bytes, x_scale, pred, w_enc, b_enc, w_pred,
     units = uunits[:HEAD]
     rest = uunits[HEAD:]
     for n in range(len(tunits)):
-        units.append(tunits[n])
         units.extend(rest[n * len(rest) // len(tunits):(n + 1) * len(rest) // len(tunits)])
+        units.append(tunits[n])
 
     with ExitStack() as ctx:
         keep = ctx.enter_context(tc.tile_pool(name="keep", bufs=1))
@@ -94,13 +95,13 @@ def tile_jointnetwork_t_kernel(tc, x_bytes, x_scale, pred, w_enc, b_enc, w_pred,
         x_c = [keep.tile([P, P], U32, name="x_c%d" % b, align_bytes=64) for b in range(B)]
         x_s = [keep.tile([P, P], U8, name="x_s%d" % b, align_bytes=64) for b in range(B)]
         p_nat = keep.tile([P, K], F32, name="p_nat", align_bytes=64)
-        e_nat = {b: keep.tile([P, K], F32, name="e_nat%d" % b, align_bytes=64) for b in (2, 3)}
-        e_rep = {b: [keep.tile([P, 2, K], F32, name="e_rep%d%d" % (b, h), align_bytes=64) for h in range(4)] for b in (2, 3)}
-        p_rep = {b: keep.tile([P, 4, K], F32, name="p_rep%d" % b, align_bytes=64) for b in (2, 3)}
+        e_nat = {b: keep.tile([P, K], F32, name="e_nat%d" % b, align_bytes=64) for b in (3,)}
+        e_rep = {b: [keep.tile([P, 2, K], F32, name="e_rep%d%d" % (b, h), align_bytes=64) for h in range(4)] for b in (3,)}
+        p_rep = {b: keep.tile([P, 4, K], F32, name="p_rep%d" % b, align_bytes=64) for b in (3,)}
         enc_ps = [None] * B
 
         def turn(src, name):
-            xt = psum.tile([P, 2, P], F32, name=name, tag="sum", bufs=4)
+            xt = psum.tile([P, 2, P], F32, name=name, tag="sum", bufs=3)
             words = src.bitcast(F32)
             for w in range(2):
                 nc.tensor.transpose(xt[:, w, :], words[:, w:2 * P:2], ident[:])
@@ -136,7 +137,6 @@ def tile_jointnetwork_t_kernel(tc, x_bytes, x_scale, pred, w_enc, b_enc, w_pred,
             return out[B - 1, 16 * q:16 * (q + 1), :, :].rearrange("t (a c) v -> (t a) (c v)", c=4)
 
         nc.scalar.copy(out=x_bf[:, 0, :], in_=bytes_in[:, 0, :].bitcast(FP8))
-        nc.scalar.copy(out=x_bf[:, 1:, :].rearrange("p b k -> p (b k)"), in_=bytes_in[:, 1:, :].rearrange("p b k -> p (b k)").bitcast(FP8))
         xt0 = turn(x_bf[:, 0, :], "xt0")
         x_product(0, xt0)
         xtp = turn(pred_sb[:], "xtp")
@@ -152,35 +152,36 @@ def tile_jointnetwork_t_kernel(tc, x_bytes, x_scale, pred, w_enc, b_enc, w_pred,
         quant(we_c[:, 1, :], we_s[:, 1, :], we_int[:, 1].rearrange("p m j -> p (m j)"))
         w_plane(nc.vector.tensor_copy, wp_raw, wp_int, 0)
         w_plane(nc.vector.tensor_copy, wp_raw, wp_int, 1)
+        w_plane(nc.scalar.copy, wp_raw, wp_int, 2)
         w_plane(nc.scalar.copy, wp_raw, wp_int, 3)
+        nc.scalar.copy(out=x_bf[:, 1:, :].rearrange("p b k -> p (b k)"), in_=bytes_in[:, 1:, :].rearrange("p b k -> p (b k)").bitcast(FP8))
         quant(we_c[:, 2, :], we_s[:, 2, :], we_int[:, 2].rearrange("p m j -> p (m j)"))
         quant(wp_c[:, 0, :], wp_s[:, 0, :], wp_int[:, 0].rearrange("p m j -> p (m j)"))
-        w_plane(nc.vector.tensor_copy, wp_raw, wp_int, 2)
         quant(we_c[:, 3, :], we_s[:, 3, :], we_int[:, 3].rearrange("p m j -> p (m j)"))
         quant(wp_c[:, 1, :], wp_s[:, 1, :], wp_int[:, 1].rearrange("p m j -> p (m j)"))
         quant(wp_c[:, 2, :], wp_s[:, 2, :], wp_int[:, 2].rearrange("p m j -> p (m j)"))
         quant(wp_c[:, 3, :], wp_s[:, 3, :], wp_int[:, 3].rearrange("p m j -> p (m j)"))
-        x_matmul(0)
-        pp = psum.tile([P, J, P], F32, name="pp", tag="sum", bufs=4)
+        pp = psum.tile([P, J, P], F32, name="pp", tag="sum", bufs=3)
         for t in range(J):
             mx(pp, t, wp_c, wp_s, pred_c[:], pred_s[:])
+        x_matmul(0)
         nc.vector.tensor_tensor(out=pred_b[:], in0=pp[:], in1=bsum[:].unsqueeze(2).to_broadcast([P, J, P]), op=ALU.add)
-        pn = psum.tile([P, J, P], F32, name="pn", tag="sum", bufs=4)
-        xt2 = turn(x_bf[:, 2, :], "xt2")
+        pn = psum.tile([P, J, P], F32, name="pn", tag="sum", bufs=3)
+        xt3 = turn(x_bf[:, 3, :], "xt3")
         for t in range(J):
             nc.tensor.transpose(pn[:, t, :], pred_b[:, t, :], ident[:])
-        x_product(2, xt2)
+        x_product(3, xt3)
         nc.vector.tensor_copy(out=p_nat[:], in_=pn[:].rearrange("p j m -> p (j m)"))
         nc.sync.dma_start(out=scratch(5), in_=p_nat[:])
-        x_quant(2)
+        x_quant(3)
         nc.vector.tensor_copy(out=wo_int[:], in_=wo_raw[:].rearrange("p j v -> p v j"))
 
         def natural(b):
-            en = psum.tile([P, K], F32, name="en%d" % b, tag="sum", bufs=4)
+            en = psum.tile([P, K], F32, name="en%d" % b, tag="sum", bufs=3)
             nc.tensor.matmul_mx(out=en[:], lhsT=x_c[b][:].bitcast(FP8X4), lhsT_scale=x_s[b][:],
                                 rhs=we_c[:].rearrange("p t m -> p (t m)").bitcast(FP8X4), rhs_scale=we_s[:].rearrange("p t m -> p (t m)"), start=True, stop=True)
             nc.vector.tensor_copy(out=e_nat[b][:], in_=en[:])
-            nc.sync.dma_start(out=scratch(4 + b), in_=e_nat[b][:])
+            nc.sync.dma_start(out=scratch(7), in_=e_nat[b][:])
 
         ORDER = (0, 4, 1, 5, 2, 6, 3, 7)
 
@@ -191,7 +192,7 @@ def tile_jointnetwork_t_kernel(tc, x_bytes, x_scale, pred, w_enc, b_enc, w_pred,
 
         def rep_e(b, h):
             for ul in ORDER:
-                nc.sync.dma_start(out=e_rep[b][h][ul:P:8], in_=scratch(4 + b).rearrange("(tb tl) k -> tl tb k", tl=16)[:, 2 * h:2 * h + 2])
+                nc.sync.dma_start(out=e_rep[b][h][ul:P:8], in_=scratch(7).rearrange("(tb tl) k -> tl tb k", tl=16)[:, 2 * h:2 * h + 2])
 
         planes, inter, codes, scales, acc, res, sums = {}, {}, {}, {}, {}, {}, {}
 
@@ -201,7 +202,7 @@ def tile_jointnetwork_t_kernel(tc, x_bytes, x_scale, pred, w_enc, b_enc, w_pred,
             if kind == "u":
                 return
             s = s0 + x
-            sums[q] = psum.tile([P, J, P], F32, name="sums", tag="sum", bufs=4)
+            sums[q] = psum.tile([P, J, P], F32, name="sums", tag="sum", bufs=3)
             for j in range(J):
                 cols = slice(j * P, (j + 1) * P)
                 nc.tensor.matmul(sums[q][:, j, :], lhsT=e_rep[b][tb // 2][:, tb % 2, cols], rhs=ident[:], start=True, stop=False, is_transpose=True)
@@ -212,33 +213,33 @@ def tile_jointnetwork_t_kernel(tc, x_bytes, x_scale, pred, w_enc, b_enc, w_pred,
             kind, b, tb, u0, n = groups[i]
             if kind == "u":
                 if x == 0:
-                    planes[i] = stage.tile([P, J, 4, T], BF16, name="planes", tag="planes", bufs=3, align_bytes=64)
+                    planes[i] = stage.tile([P, J, 4, T], BF16, name="planes", tag="planes", bufs=5, align_bytes=64)
                 for j in range(J):
                     nc.scalar.activation(out=planes[i][:, j, x, :], in_=enc_ps[b][:, j, :], func=ACT.Tanh,
                                          bias=pred_b[:, j, b * U + u0 + x:b * U + u0 + x + 1])
             else:
                 if x == 0:
-                    inter[i] = stage.tile([P, 4 * T, J], BF16, name="inter", tag="inter", bufs=4, align_bytes=64)
+                    inter[i] = stage.tile([P, 4 * T, J], BF16, name="inter", tag="inter", bufs=8, align_bytes=64)
                 nc.scalar.activation(out=inter[i][:, x * T:(x + 1) * T, :], in_=sums[q][:].rearrange("p j n -> p n j"), func=ACT.Tanh)
 
         def interleave(i):
             kind, b, tb, u0, n = groups[i]
             if kind == "t":
                 return
-            inter[i] = stage.tile([P, 4 * T, J], BF16, name="inter", tag="inter", bufs=4, align_bytes=64)
+            inter[i] = stage.tile([P, 4 * T, J], BF16, name="inter", tag="inter", bufs=8, align_bytes=64)
             dst = inter[i][:, :n * T, :]
             src = planes[i][:].rearrange("p j u t -> p j (u t)")[:, :, :n * T]
             nc.vector.tensor_copy(out=dst.rearrange("p (c i) j -> p c j i", i=4), in_=src.rearrange("p j (c i) -> p c j i", i=4))
 
         def quantise(i):
             n = groups[i][4]
-            codes[i] = stage.tile([P, 4 * T], U32, name="codes", tag="codes", bufs=3, align_bytes=64)
-            scales[i] = stage.tile([P, 4 * T], U8, name="scales", tag="scales", bufs=3, align_bytes=64)
+            codes[i] = stage.tile([P, 4 * T], U32, name="codes", tag="codes", bufs=4, align_bytes=64)
+            scales[i] = stage.tile([P, 4 * T], U8, name="scales", tag="scales", bufs=4, align_bytes=64)
             quant(codes[i][:, :n * T], scales[i][:, :n * T], inter[i][:, :n * T, :].rearrange("p c j -> p (c j)"))
 
         def multiply(i):
             n = groups[i][4]
-            acc[i] = psum.tile([P, 4, V], F32, name="acc", tag="acc", bufs=2)
+            acc[i] = psum.tile([P, 4, V], F32, name="acc", tag="acc", bufs=3)
             for u in range(n):
                 cols = slice(u * T, (u + 1) * T)
                 nc.tensor.matmul_mx(out=acc[i][:, u, :], lhsT=codes[i][:, cols].bitcast(FP8X4), lhsT_scale=scales[i][:, cols],
@@ -246,7 +247,7 @@ def tile_jointnetwork_t_kernel(tc, x_bytes, x_scale, pred, w_enc, b_enc, w_pred,
 
         def add_bias(i):
             n = groups[i][4]
-            res[i] = stage.tile([P, 4, V], F32, name="res", tag="res", bufs=4, align_bytes=64)
+            res[i] = stage.tile([P, 4, V], F32, name="res", tag="res", bufs=6, align_bytes=64)
             nc.vector.tensor_tensor(out=res[i][:, :n, :], in0=acc[i][:, :n, :], in1=bo[:].unsqueeze(1).to_broadcast([P, n, V]), op=ALU.add)
 
         def clip_store(i):
@@ -267,25 +268,22 @@ def tile_jointnetwork_t_kernel(tc, x_bytes, x_scale, pred, w_enc, b_enc, w_pred,
         def at(slot, order, *task):
             slots.setdefault(slot, []).append((order, len(slots.get(slot, [])), task))
 
-        at(0, 0, natural, 2)
-        at(0, 1, rep_p, 2)
-        at(0, 2, rep_e, 2, 0)
-        at(1, 0, side, 3)
-        at(2, 0, x_quant, 3)
-        at(2, 1, natural, 3)
-        at(4, 0, side, 1)
-        at(5, 0, x_quant, 1)
-        at(5, 1, x_matmul, 1)
+        at(0, 0, natural, 3)
+        at(0, 1, rep_p, 3)
+        at(0, 2, rep_e, 3, 0)
+        at(6, 0, side, 1)
+        at(7, 0, x_quant, 1)
+        at(7, 1, x_matmul, 1)
+        at(12, 0, side, 2)
+        at(13, 0, x_quant, 2)
+        free = max(q for q in range(len(units)) if units[q][0] < len(sizes[0])) + 2
+        at(free, 1, x_matmul, 2)
         at(1, 5, lambda z: quant(wo_c[:], wo_s[:], wo_int[:].rearrange("p v j -> p (v j)")), 0)
         sumq = [q for q in range(len(units)) if groups[units[q][0]][0] == "t"]
-        for h in range(1, 8):
-            b = 2 + h // 4
-            slot = max(3, sumq[8 * h] - 16)
-            if h == 4:
-                at(slot, 6, rep_p, b)
-            at(slot, 7, rep_e, b, h % 4)
+        for h in range(1, 4):
+            at(max(3, sumq[8 * h] - 24), 7, rep_e, 3, h)
         done = 0
-        for q in range(len(units) + 8):
+        for q in range(len(units) + 16):
             if q < len(units):
                 i, x = units[q]
                 while done < len(sumq) and sumq[done] <= q + LOOK:
@@ -297,8 +295,8 @@ def tile_jointnetwork_t_kernel(tc, x_bytes, x_scale, pred, w_enc, b_enc, w_pred,
                     if late:
                         at(q + 1, 2, interleave, i)
                     at(q + 1 + late, 3, quantise, i)
-                    at(q + 1 + late, 4, multiply, i)
-                    at(q + 3 + late, 1, add_bias, i)
-                    at(q + 3 + 1 + late, 0, clip_store, i)
+                    at(q + 4 + late, 4, multiply, i)
+                    at(q + 8 + late, 1, add_bias, i)
+                    at(q + 8 + 1 + late, 0, clip_store, i)
             for order, seq, task in sorted(slots.get(q, []), key=lambda z: z[:2]):
                 task[0](*task[1:])

from contextlib import ExitStack

import concourse.mybir as mybir
from concourse.masks import make_identity

F32 = mybir.dt.float32
BF16 = mybir.dt.bfloat16
U32 = mybir.dt.uint32
U8 = mybir.dt.uint8
FP8 = mybir.dt.float8_e4m3fn
FP8X4 = mybir.dt.float8_e4m3fn_x4
ALU = mybir.AluOpType
ACT = mybir.ActivationFunctionType

P = 128
J = 4
B, T, U, K, V = 4, 128, 32, 512, 128
LIMIT = 15.0
FLOPS = 2 * (B * T * K * K + B * U * K * K + B * T * U * K * V)
LOOK = 6
HEAD = 24


def tile_jointnetwork_t_kernel(tc, x_bytes, x_scale, pred, w_enc, b_enc, w_pred, b_pred, w_out, b_out, out):
    nc = tc.nc
    sizes = [[1, 1, 2, 4, 4, 4, 4, 4, 4, 4], [4] * 8, [4] * 7 + [2, 1, 1]]
    ugroups = []
    for b in range(3):
        u = 0
        for n in sizes[b]:
            ugroups.append(("u", b, 0, u, n))
            u += n
    tgroups = [("t", 3, i, 0, 4) for i in range(7)]
    for s0, n in ((0, 2), (2, 1), (3, 1)):
        tgroups.append(("t", 3, 7, s0, n))
    groups = ugroups + tgroups
    ngroups = len(groups)
    uunits = [(i, x) for i in range(len(ugroups)) for x in range(groups[i][4])]
    tunits = [(i, x) for i in range(len(ugroups), ngroups) for x in range(groups[i][4])]
    units = uunits[:HEAD]
    rest = uunits[HEAD:]
    for n in range(len(tunits)):
        units.extend(rest[n * len(rest) // len(tunits):(n + 1) * len(rest) // len(tunits)])
        units.append(tunits[n])

    with ExitStack() as ctx:
        keep = ctx.enter_context(tc.tile_pool(name="keep", bufs=1))
        stage = ctx.enter_context(tc.tile_pool(name="stage", bufs=3))
        psum = ctx.enter_context(tc.psum_pool(name="psum", bufs=1))
        ctx.enter_context(tc.manual_schedule())

        scale = keep.tile([P, J], F32, name="scale")
        nc.sync.dma_start(out=scale[:], in_=x_scale.rearrange("o q (p j) -> p (o q j)", j=J))
        bytes_in = keep.tile([P, B, K], U8, name="bytes_in", align_bytes=64)
        nc.sync.dma_start(out=bytes_in[:], in_=x_bytes.rearrange("b t k -> t b k"))
        pred_sb = keep.tile([P, K], BF16, name="pred_sb", align_bytes=64)
        nc.sync.dma_start(out=pred_sb[:], in_=pred.rearrange("b u k -> (b u) k"))
        we_raw = keep.tile([P, J, K], BF16, name="we_raw", align_bytes=64)
        nc.sync.dma_start(out=we_raw[:], in_=w_enc.rearrange("(p j) c -> p j c", j=J))
        wp_raw = keep.tile([P, J, K], BF16, name="wp_raw", align_bytes=64)
        nc.sync.dma_start(out=wp_raw[:], in_=w_pred.rearrange("(p j) c -> p j c", j=J))
        wo_raw = keep.tile([P, J, V], BF16, name="wo_raw", align_bytes=64)
        nc.sync.dma_start(out=wo_raw[:], in_=w_out.rearrange("(p j) v -> p j v", j=J))
        be = keep.tile([P, J], BF16, name="be")
        nc.gpsimd.dma_start(out=be[:], in_=b_enc.rearrange("(p j) -> p j", j=J))
        bp = keep.tile([P, J], BF16, name="bp")
        nc.gpsimd.dma_start(out=bp[:], in_=b_pred.rearrange("(p j) -> p j", j=J))
        bo = keep.tile([P, V], BF16, name="bo")

        ident = keep.tile([P, P], F32, name="ident", align_bytes=64)
        make_identity(nc, ident[:])
        nc.gpsimd.dma_start(out=bo[:], in_=b_out.partition_broadcast(P))

        warm = keep.tile([P, 1], F32, name="warm")
        nc.vector.memset(warm[:], 0.0)
        warm2 = keep.tile([P, 1], F32, name="warm2")
        nc.scalar.activation(out=warm2[:], in_=warm[:], func=ACT.Tanh)

        we_int = keep.tile([P, J, P, J], BF16, name="we_int", align_bytes=64)
        we_c = keep.tile([P, J, P], U32, name="we_c", align_bytes=64)
        we_s = keep.tile([P, J, P], U8, name="we_s", align_bytes=64)
        wp_int = keep.tile([P, J, P, J], BF16, name="wp_int", align_bytes=64)
        wp_c = keep.tile([P, J, P], U32, name="wp_c", align_bytes=64)
        wp_s = keep.tile([P, J, P], U8, name="wp_s", align_bytes=64)
        wo_int = keep.tile([P, V, J], BF16, name="wo_int", align_bytes=64)
        wo_c = keep.tile([P, V], U32, name="wo_c", align_bytes=64)
        wo_s = keep.tile([P, V], U8, name="wo_s", align_bytes=64)
        bsum = keep.tile([P, J], F32, name="bsum")
        pred_b = keep.tile([P, J, P], F32, name="pred_b", align_bytes=64)
        pred_int = keep.tile([P, P, J], BF16, name="pred_int", align_bytes=64)
        pred_c = keep.tile([P, P], U32, name="pred_c", align_bytes=64)
        pred_s = keep.tile([P, P], U8, name="pred_s", align_bytes=64)
        x_bf = keep.tile([P, B, K], BF16, name="x_bf", align_bytes=64)
        x_int = [keep.tile([P, P, J], BF16, name="x_int%d" % b, align_bytes=64) for b in range(B)]
        x_c = [keep.tile([P, P], U32, name="x_c%d" % b, align_bytes=64) for b in range(B)]
        x_s = [keep.tile([P, P], U8, name="x_s%d" % b, align_bytes=64) for b in range(B)]
        p_nat = keep.tile([P, K], F32, name="p_nat", align_bytes=64)
        e_nat = {b: keep.tile([P, K], F32, name="e_nat%d" % b, align_bytes=64) for b in (3,)}
        e_rep = {b: [keep.tile([P, 2, K], F32, name="e_rep%d%d" % (b, h), align_bytes=64) for h in range(4)] for b in (3,)}
        p_rep = {b: keep.tile([P, 4, K], F32, name="p_rep%d" % b, align_bytes=64) for b in (3,)}
        enc_ps = [None] * B

        def turn(src, name):
            xt = psum.tile([P, 2, P], F32, name=name, tag="sum", bufs=3)
            words = src.bitcast(F32)
            for w in range(2):
                nc.tensor.transpose(xt[:, w, :], words[:, w:2 * P:2], ident[:])
            return xt

        def w_plane(engine_copy, raw, dst, t):
            engine_copy(out=dst[:, t], in_=raw[:].rearrange("p j (m t) -> p t m j", t=J)[:, t])

        def quant(c, s, src):
            nc.vector.quantize_mx(out=c.bitcast(FP8X4), scales=s, in_=src)

        def x_product(b, xt):
            nc.vector.tensor_tensor(
                out=x_int[b][:].rearrange("p r (w e) -> p r w e", e=2),
                in0=xt[:].rearrange("p w r -> p (w r)").bitcast(BF16).rearrange("p (w r e) -> p r w e", w=2, e=2),
                in1=scale[:].rearrange("p (w e) -> p w e", e=2).unsqueeze(1).to_broadcast([P, P, 2, 2]),
                op=ALU.mult,
            )

        def x_quant(b):
            quant(x_c[b][:], x_s[b][:], x_int[b][:].rearrange("p r j -> p (r j)"))

        def mx(ps, t, wc, ws, c, s):
            nc.tensor.matmul_mx(out=ps[:, t, :], lhsT=wc[:, t, :].bitcast(FP8X4), lhsT_scale=ws[:, t, :],
                                rhs=c.bitcast(FP8X4), rhs_scale=s, start=True, stop=True)

        def x_matmul(b):
            enc_ps[b] = psum.tile([P, J, P], F32, name="enc%d" % b, tag="enc", bufs=2)
            for t in range(J):
                mx(enc_ps[b], t, we_c, we_s, x_c[b][:], x_s[b][:])

        def scratch(q):
            return out[B - 1, 16 * q:16 * (q + 1), :, :].rearrange("t (a c) v -> (t a) (c v)", c=4)

        nc.scalar.copy(out=x_bf[:, 0, :], in_=bytes_in[:, 0, :].bitcast(FP8))
        xt0 = turn(x_bf[:, 0, :], "xt0")
        x_product(0, xt0)
        xtp = turn(pred_sb[:], "xtp")
        nc.vector.tensor_tensor(out=bsum[:], in0=be[:], in1=bp[:], op=ALU.add)
        x_quant(0)
        nc.scalar.copy(out=pred_int[:].rearrange("p r j -> p (r j)").bitcast(F32).rearrange("p (r w) -> p r w", w=2), in_=xtp[:].rearrange("p w r -> p r w"))
        w_plane(nc.vector.tensor_copy, we_raw, we_int, 0)
        w_plane(nc.vector.tensor_copy, we_raw, we_int, 1)
        w_plane(nc.scalar.copy, we_raw, we_int, 2)
        w_plane(nc.scalar.copy, we_raw, we_int, 3)
        quant(we_c[:, 0, :], we_s[:, 0, :], we_int[:, 0].rearrange("p m j -> p (m j)"))
        quant(pred_c[:], pred_s[:], pred_int[:].rearrange("p r j -> p (r j)"))
        quant(we_c[:, 1, :], we_s[:, 1, :], we_int[:, 1].rearrange("p m j -> p (m j)"))
        w_plane(nc.vector.tensor_copy, wp_raw, wp_int, 0)
        w_plane(nc.vector.tensor_copy, wp_raw, wp_int, 1)
        w_plane(nc.scalar.copy, wp_raw, wp_int, 2)
        w_plane(nc.scalar.copy, wp_raw, wp_int, 3)
        nc.scalar.copy(out=x_bf[:, 1:, :].rearrange("p b k -> p (b k)"), in_=bytes_in[:, 1:, :].rearrange("p b k -> p (b k)").bitcast(FP8))
        quant(we_c[:, 2, :], we_s[:, 2, :], we_int[:, 2].rearrange("p m j -> p (m j)"))
        quant(wp_c[:, 0, :], wp_s[:, 0, :], wp_int[:, 0].rearrange("p m j -> p (m j)"))
        quant(we_c[:, 3, :], we_s[:, 3, :], we_int[:, 3].rearrange("p m j -> p (m j)"))
        quant(wp_c[:, 1, :], wp_s[:, 1, :], wp_int[:, 1].rearrange("p m j -> p (m j)"))
        quant(wp_c[:, 2, :], wp_s[:, 2, :], wp_int[:, 2].rearrange("p m j -> p (m j)"))
        quant(wp_c[:, 3, :], wp_s[:, 3, :], wp_int[:, 3].rearrange("p m j -> p (m j)"))
        pp = psum.tile([P, J, P], F32, name="pp", tag="sum", bufs=3)
        for t in range(J):
            mx(pp, t, wp_c, wp_s, pred_c[:], pred_s[:])
        x_matmul(0)
        nc.vector.tensor_tensor(out=pred_b[:], in0=pp[:], in1=bsum[:].unsqueeze(2).to_broadcast([P, J, P]), op=ALU.add)
        pn = psum.tile([P, J, P], F32, name="pn", tag="sum", bufs=3)
        xt3 = turn(x_bf[:, 3, :], "xt3")
        for t in range(J):
            nc.tensor.transpose(pn[:, t, :], pred_b[:, t, :], ident[:])
        x_product(3, xt3)
        nc.vector.tensor_copy(out=p_nat[:], in_=pn[:].rearrange("p j m -> p (j m)"))
        nc.sync.dma_start(out=scratch(5), in_=p_nat[:])
        x_quant(3)
        nc.vector.tensor_copy(out=wo_int[:], in_=wo_raw[:].rearrange("p j v -> p v j"))

        def natural(b):
            en = psum.tile([P, K], F32, name="en%d" % b, tag="sum", bufs=3)
            nc.tensor.matmul_mx(out=en[:], lhsT=x_c[b][:].bitcast(FP8X4), lhsT_scale=x_s[b][:],
                                rhs=we_c[:].rearrange("p t m -> p (t m)").bitcast(FP8X4), rhs_scale=we_s[:].rearrange("p t m -> p (t m)"), start=True, stop=True)
            nc.vector.tensor_copy(out=e_nat[b][:], in_=en[:])
            nc.sync.dma_start(out=scratch(7), in_=e_nat[b][:])

        ORDER = (0, 4, 1, 5, 2, 6, 3, 7)

        def rep_p(b):
            rows = scratch(5).rearrange("(b ul s) k -> b ul (s k)", b=B, s=4)
            for ul in ORDER:
                nc.sync.dma_start(out=p_rep[b][ul:P:8].rearrange("p s k -> p (s k)"), in_=rows[b, ul].partition_broadcast(16))

        def rep_e(b, h):
            for ul in ORDER:
                nc.sync.dma_start(out=e_rep[b][h][ul:P:8], in_=scratch(7).rearrange("(tb tl) k -> tl tb k", tl=16)[:, 2 * h:2 * h + 2])

        planes, inter, codes, scales, acc, res, sums = {}, {}, {}, {}, {}, {}, {}

        def sum_unit(q):
            i, x = units[q]
            kind, b, tb, s0, n = groups[i]
            if kind == "u":
                return
            s = s0 + x
            sums[q] = psum.tile([P, J, P], F32, name="sums", tag="sum", bufs=3)
            for j in range(J):
                cols = slice(j * P, (j + 1) * P)
                nc.tensor.matmul(sums[q][:, j, :], lhsT=e_rep[b][tb // 2][:, tb % 2, cols], rhs=ident[:], start=True, stop=False, is_transpose=True)
                nc.tensor.matmul(sums[q][:, j, :], lhsT=p_rep[b][:, s, cols], rhs=ident[:], start=False, stop=True, is_transpose=True)

        def tanh_unit(q):
            i, x = units[q]
            kind, b, tb, u0, n = groups[i]
            if kind == "u":
                if x == 0:
                    planes[i] = stage.tile([P, J, 4, T], BF16, name="planes", tag="planes", bufs=5, align_bytes=64)
                for j in range(J):
                    nc.scalar.activation(out=planes[i][:, j, x, :], in_=enc_ps[b][:, j, :], func=ACT.Tanh,
                                         bias=pred_b[:, j, b * U + u0 + x:b * U + u0 + x + 1])
            else:
                if x == 0:
                    inter[i] = stage.tile([P, 4 * T, J], BF16, name="inter", tag="inter", bufs=8, align_bytes=64)
                nc.scalar.activation(out=inter[i][:, x * T:(x + 1) * T, :], in_=sums[q][:].rearrange("p j n -> p n j"), func=ACT.Tanh)

        def interleave(i):
            kind, b, tb, u0, n = groups[i]
            if kind == "t":
                return
            inter[i] = stage.tile([P, 4 * T, J], BF16, name="inter", tag="inter", bufs=8, align_bytes=64)
            dst = inter[i][:, :n * T, :]
            src = planes[i][:].rearrange("p j u t -> p j (u t)")[:, :, :n * T]
            nc.vector.tensor_copy(out=dst.rearrange("p (c i) j -> p c j i", i=4), in_=src.rearrange("p j (c i) -> p c j i", i=4))

        def quantise(i):
            n = groups[i][4]
            codes[i] = stage.tile([P, 4 * T], U32, name="codes", tag="codes", bufs=4, align_bytes=64)
            scales[i] = stage.tile([P, 4 * T], U8, name="scales", tag="scales", bufs=4, align_bytes=64)
            quant(codes[i][:, :n * T], scales[i][:, :n * T], inter[i][:, :n * T, :].rearrange("p c j -> p (c j)"))

        def multiply(i):
            n = groups[i][4]
            acc[i] = psum.tile([P, 4, V], F32, name="acc", tag="acc", bufs=3)
            for u in range(n):
                cols = slice(u * T, (u + 1) * T)
                nc.tensor.matmul_mx(out=acc[i][:, u, :], lhsT=codes[i][:, cols].bitcast(FP8X4), lhsT_scale=scales[i][:, cols],
                                    rhs=wo_c[:].bitcast(FP8X4), rhs_scale=wo_s[:], start=True, stop=True)

        def add_bias(i):
            n = groups[i][4]
            res[i] = stage.tile([P, 4, V], F32, name="res", tag="res", bufs=6, align_bytes=64)
            nc.vector.tensor_tensor(out=res[i][:, :n, :], in0=acc[i][:, :n, :], in1=bo[:].unsqueeze(1).to_broadcast([P, n, V]), op=ALU.add)

        def clip_store(i):
            kind, b, tb, u0, n = groups[i]
            nc.vector.tensor_scalar(out=res[i][:, :n, :], in0=res[i][:, :n, :], scalar1=LIMIT, scalar2=-LIMIT, op0=ALU.min, op1=ALU.max)
            if kind == "u":
                dst = out[b, :, u0:u0 + n, :]
            else:
                dst = out[b, 16 * tb:16 * (tb + 1), :, :].rearrange("t (a c) v -> (t a) c v", c=4)[:, u0:u0 + n, :]
            nc.sync.dma_start(out=dst, in_=res[i][:, :n, :])

        def side(b):
            xtb = turn(x_bf[:, b, :], "xt%d" % b)
            x_product(b, xtb)

        slots = {}

        def at(slot, order, *task):
            slots.setdefault(slot, []).append((order, len(slots.get(slot, [])), task))

        at(0, 0, natural, 3)
        at(0, 1, rep_p, 3)
        at(0, 2, rep_e, 3, 0)
        at(6, 0, side, 1)
        at(7, 0, x_quant, 1)
        at(7, 1, x_matmul, 1)
        at(12, 0, side, 2)
        at(13, 0, x_quant, 2)
        free = max(q for q in range(len(units)) if units[q][0] < len(sizes[0])) + 2
        at(free, 1, x_matmul, 2)
        at(1, 5, lambda z: quant(wo_c[:], wo_s[:], wo_int[:].rearrange("p v j -> p (v j)")), 0)
        sumq = [q for q in range(len(units)) if groups[units[q][0]][0] == "t"]
        for h in range(1, 4):
            at(max(3, sumq[8 * h] - 24), 7, rep_e, 3, h)
        done = 0
        for q in range(len(units) + 16):
            if q < len(units):
                i, x = units[q]
                while done < len(sumq) and sumq[done] <= q + LOOK:
                    sum_unit(sumq[done])
                    done += 1
                tanh_unit(q)
                if x == groups[i][4] - 1:
                    late = 1 if groups[i][0] == "u" else 0
                    if late:
                        at(q + 1, 2, interleave, i)
                    at(q + 1 + late, 3, quantise, i)
                    at(q + 4 + late, 4, multiply, i)
                    at(q + 8 + late, 1, add_bias, i)
                    at(q + 8 + 1 + late, 0, clip_store, i)
            for order, seq, task in sorted(slots.get(q, []), key=lambda z: z[:2]):
                task[0](*task[1:])
